import numpy as np
import ml_dtypes


def mxq(x, axis, fmt="e4m3"):
    dtype, down = {"e4m3": (ml_dtypes.float8_e4m3fn, 7), "e5m2": (ml_dtypes.float8_e5m2, 14)}[fmt]
    v = np.moveaxis(np.asarray(x, np.float32).astype(ml_dtypes.bfloat16).astype(np.float64), axis, -1)
    blocks = v.reshape(v.shape[:-1] + (-1, 32))
    amax = np.abs(blocks).max(-1, keepdims=True)
    byte = np.maximum(np.where(amax > 0, np.frexp(amax)[1] - 1 + 127, 0) - down, 1)
    scale = np.exp2(byte - 127.0)
    codes = (blocks / scale).astype(np.float32).astype(dtype).astype(np.float64)
    return np.moveaxis((codes * scale).reshape(v.shape), -1, axis)


WIDE = False


def mx_kscale(k):
    if not WIDE:
        return np.ones(k)
    levels = np.array([10, -10, 5, -5, 0])
    a = np.random.permutation(np.resize(levels, k // 512 * 4)).reshape(k // 512, 4)
    idx = np.arange(k)
    return np.exp2(a[idx // 512, idx % 128 // 32])


BF16 = ml_dtypes.bfloat16


def bf(x):
    return np.asarray(x, np.float32).astype(BF16)


def f64(x):
    return np.asarray(x).astype(np.float64)


E2M1 = np.array([0.0, 0.5, 1.0, 1.5, 2.0, 3.0, 4.0, 6.0, -0.0, -0.5, -1.0, -1.5, -2.0, -3.0, -4.0, -6.0])


def pack_weight(w, fmt):
    k, n = w.shape
    w = f64(bf(w)).reshape(k // 32, 32, n)
    amax = np.abs(w).max(1)
    if fmt == "e4m3":
        byte = np.frexp(amax)[1] - 1 + 127 - 7
    else:
        mant, ex = np.frexp(amax / 6.0)
        byte = np.where(mant > 0.5, ex, ex - 1) + 127
    byte = np.clip(np.where(amax > 0, byte, 1), 1, 254)
    scaled = (w * np.exp2(127.0 - byte)[:, None, :]).reshape(k, n).astype(np.float32)
    by_word = np.ascontiguousarray(scaled.reshape(k // 512, 128, 4, n).transpose(0, 1, 3, 2))
    if fmt == "e4m3":
        words = by_word.astype(ml_dtypes.float8_e4m3fn).view(np.uint8)
    else:
        c = by_word.astype(ml_dtypes.float4_e2m1fn).view(np.uint8) & 0xF
        words = c[..., 0::2] | (c[..., 1::2] << 4)
    return np.ascontiguousarray(words), np.ascontiguousarray(byte.astype(np.uint8).reshape(k // 512, 16, n))


def unpack_weight(words, scales, fmt):
    g, p, n, _ = words.shape
    if fmt == "e4m3":
        vals = np.ascontiguousarray(words).view(ml_dtypes.float8_e4m3fn).astype(np.float64)
    else:
        nib = np.empty((g, p, n, 4), np.uint8)
        nib[..., 0::2] = words & 0xF
        nib[..., 1::2] = words >> 4
        vals = E2M1[nib]
    vals = vals * np.repeat(np.exp2(scales.astype(np.float64) - 127.0), 8, axis=1)[..., None]
    return vals.transpose(0, 1, 3, 2).reshape(g * 512, n)


B, S, D, H, DH, F = 2, 64, 8192, 16, 64, 2048
E = H * DH
EPS = 1e-5
NTERMS = 120
FMT = "e4m3"


def layernorm(x, g, b):
    mu = x.mean(-1, keepdims=True)
    var = np.square(x - mu).mean(-1, keepdims=True)
    return (x - mu) / np.sqrt(var + EPS) * g + b


def erf(v):
    a = np.minimum(np.maximum(v, -6.0), 6.0)
    term = a.copy()
    total = a.copy()
    for n in range(1, NTERMS):
        term = term * (2.0 * a * a) / (2.0 * n + 1.0)
        total = total + term
    return 2.0 / np.sqrt(np.pi) * np.exp(-a * a) * total


def gelu_erf(v):
    return 0.5 * v * (1.0 + erf(v / np.sqrt(2.0)))


def setup_inputs():
    s, t = mx_kscale(E), mx_kscale(D)
    x = np.random.standard_normal((B, S, D)) + 0.5 * np.random.standard_normal((B, S, 1))
    h_attn = bf(0.2 * np.random.standard_normal((B, S, E)) * s)
    w_out = np.random.standard_normal((D, E)) * 2.0 / np.sqrt(E) / s
    w_fc1 = np.random.standard_normal((F, D)) / np.sqrt(D) / t
    g2 = bf((1.0 + 0.1 * np.random.standard_normal(D)) * t)
    b2 = bf(0.1 * np.random.standard_normal(D) * t)
    w_out_words, w_out_scales = pack_weight(np.ascontiguousarray(w_out.T), FMT)
    w_fc1_words, w_fc1_scales = pack_weight(np.ascontiguousarray(w_fc1.T), FMT)
    return {"h_attn": h_attn,
            "x": bf(x),
            "w_out_words": w_out_words,
            "w_out_scales": w_out_scales,
            "w_fc1_words": w_fc1_words,
            "w_fc1_scales": w_fc1_scales,
            "g2": g2,
            "b2": b2}


def reference(h_attn, x, w_out_words, w_out_scales, w_fc1_words, w_fc1_scales, g2, b2):
    x_mid = f64(x) + (mxq(f64(h_attn), 2, "e4m3") @ unpack_weight(w_out_words, w_out_scales, FMT))
    h = layernorm(x_mid, f64(g2), f64(b2))
    u = mxq(h, 2, "e4m3") @ unpack_weight(w_fc1_words, w_fc1_scales, FMT)
    return x_mid, gelu_erf(u)

@@ -1,0 +1,265 @@
+import concourse.mybir as mybir
+from concourse.masks import make_identity
+
+F32 = mybir.dt.float32
+BF16 = mybir.dt.bfloat16
+U8 = mybir.dt.uint8
+U32 = mybir.dt.uint32
+I32 = mybir.dt.int32
+FP8X4 = mybir.dt.float8_e4m3fn_x4
+ALU = mybir.AluOpType
+ACT = mybir.ActivationFunctionType
+
+P = 128
+PACK = 4
+K_PASS = P * PACK
+E = 1024
+D = 8192
+F = 2048
+EPS = 1e-5
+BANK = 512
+OUT_GROUPS = E // K_PASS
+FC1_GROUPS = D // K_PASS
+TILE_COLS = 2048
+BANKS_PER_TILE = TILE_COLS // BANK
+OUT_QUARTERS = D // TILE_COLS
+OUT_TILES = OUT_QUARTERS * OUT_GROUPS
+ALL_TILES = OUT_TILES + FC1_GROUPS
+RING = 16
+assert OUT_TILES + RING == ALL_TILES
+PLANES = 4
+GROUPS_PER_ROUND = 4
+ROUNDS = FC1_GROUPS // GROUPS_PER_ROUND
+
+FLOPS = 2 * P * E * D + 2 * P * D * F
+
+
+def tile_minitransformerlayer_pb_k_kernel(
+    tc, h_attn, x, w_out_words, w_out_scales, w_fc1_words, w_fc1_scales, g2, b2, out_0, out_1
+):
+    nc = tc.nc
+    h_attn_rows = h_attn.flatten_outer_dims()
+    x_rows = x.flatten_outer_dims()
+    x_mid_rows = out_0.flatten_outer_dims()
+    act_rows = out_1.flatten_outer_dims()
+
+    with (
+        tc.manual_schedule(),
+        tc.tile_pool(name="keep", bufs=1) as keep,
+        tc.tile_pool(name="ring", bufs=RING) as ring,
+        tc.tile_pool(name="stage", bufs=GROUPS_PER_ROUND) as stage,
+        tc.psum_pool(name="work", bufs=4) as work,
+        tc.psum_pool(name="sums", bufs=1) as sums,
+    ):
+        ident = keep.tile([P, P], F32)
+        attn = keep.tile([P, E], BF16)
+        attn_grouped = keep.tile([P, OUT_GROUPS, P, PACK], BF16, align_bytes=64)
+        attn_codes = keep.tile([P, OUT_GROUPS, P], U32, align_bytes=64)
+        attn_scales = keep.tile([P, OUT_GROUPS, P], U8, align_bytes=64)
+        out_planes = keep.tile([P, OUT_GROUPS, TILE_COLS], U8, align_bytes=64)
+        fc1_planes = keep.tile([P, FC1_GROUPS // PLANES, F], U8, align_bytes=64)
+        gain_bias_rows = keep.tile([P, K_PASS], BF16)
+        gain_bias_sorted = keep.tile([P, PACK, P], F32)
+        gain_bias = keep.tile([P, 2 * FC1_GROUPS, PACK], F32)
+        x_sb = keep.tile([P, D], BF16)
+        x_mid = keep.tile([P, D], F32)
+        stats = keep.tile([P, D // BANK, 6], F32)
+        mean_var = keep.tile([P, 2], F32)
+        var_eps = keep.tile([P, 1], F32)
+        std = keep.tile([P, 1], F32)
+        rstd = keep.tile([P, 1], F32)
+        h_codes = keep.tile([P, FC1_GROUPS, P], U32, align_bytes=64)
+        h_scales = keep.tile([P, FC1_GROUPS, P], U8, align_bytes=64)
+        act = keep.tile([P, F], F32)
+
+        nc.vector.memset(gain_bias_rows[:], 0.0)
+        nc.vector.memset(out_planes[:].bitcast(I32), 0)
+        nc.vector.memset(fc1_planes[:].bitcast(I32), 0)
+        make_identity(nc, ident[:])
+
+        nc.sync.dma_start(out=attn[:], in_=h_attn_rows)
+        nc.sync.dma_start(
+            out=gain_bias_rows[0:FC1_GROUPS, :], in_=g2.rearrange("(g k) -> g k", k=K_PASS)
+        )
+        nc.sync.dma_start(
+            out=gain_bias_rows[FC1_GROUPS : 2 * FC1_GROUPS, :],
+            in_=b2.rearrange("(g k) -> g k", k=K_PASS),
+        )
+        for g in range(OUT_GROUPS):
+            for q in range(4):
+                nc.sync.dma_start(
+                    out=out_planes[32 * q : 32 * q + 4 * PLANES, g, :].bitcast(I32),
+                    in_=w_out_scales[g, 4 * q : 4 * q + 4, :]
+                    .rearrange("r (c n) -> c r n", c=PLANES)
+                    .bitcast(I32),
+                )
+        for j in range(FC1_GROUPS // PLANES):
+            for q in range(4):
+                nc.sync.dma_start(
+                    out=fc1_planes[32 * q : 32 * q + 4 * PLANES, j, :].bitcast(I32),
+                    in_=w_fc1_scales[PLANES * j : PLANES * (j + 1), 4 * q : 4 * q + 4, :].bitcast(I32),
+                )
+        nc.sync.dma_start(out=x_sb[:], in_=x_rows)
+
+        weights = {}
+
+        def load_weight_tile(i):
+            words = ring.tile([P, TILE_COLS], U32, align_bytes=64)
+            if i < OUT_TILES:
+                c, g = divmod(i, OUT_GROUPS)
+                source = w_out_words[g].rearrange("p n t -> p (n t)")[
+                    :, PACK * TILE_COLS * c : PACK * TILE_COLS * (c + 1)
+                ]
+            else:
+                source = w_fc1_words[i - OUT_TILES].rearrange("p n t -> p (n t)")
+            nc.sync.dma_start(out=words[:].bitcast(I32), in_=source.bitcast(I32))
+            weights[i] = words
+
+        for i in range(RING):
+            load_weight_tile(i)
+
+        attn_words = attn[:].bitcast(F32)
+        attn_t = work.tile([P, OUT_GROUPS, 2, P], F32, tag="work")
+        for g in range(OUT_GROUPS):
+            for u in range(2):
+                nc.tensor.transpose(
+                    out=attn_t[:, g, u, :],
+                    in_=attn_words[:, 256 * g + u : 256 * (g + 1) : 2],
+                    identity=ident[:],
+                )
+        nc.vector.tensor_copy(
+            out=attn_grouped[:].bitcast(F32), in_=attn_t[:].rearrange("p g u k -> p g k u")
+        )
+
+        nc.vector.tensor_copy(
+            out=gain_bias_sorted[:], in_=gain_bias_rows[:].rearrange("r (p t) -> r t p", t=PACK)
+        )
+        nc.vector.quantize_mx(
+            out=attn_codes[:].rearrange("p g k -> p (g k)").bitcast(FP8X4),
+            scales=attn_scales[:].rearrange("p g k -> p (g k)"),
+            in_=attn_grouped[:].rearrange("p g k t -> p (g k t)"),
+        )
+        gain_bias_t = work.tile([P, PACK, P], F32, tag="work")
+        for t in range(PACK):
+            nc.tensor.transpose(
+                out=gain_bias_t[:, t, :], in_=gain_bias_sorted[:, t, :], identity=ident[:]
+            )
+        nc.vector.tensor_copy(
+            out=gain_bias[:],
+            in_=gain_bias_t[:, :, 0 : 2 * FC1_GROUPS].rearrange("p t r -> p r t"),
+        )
+
+        for c in range(OUT_QUARTERS):
+            for j in range(BANKS_PER_TILE):
+                cols = slice(BANK * j, BANK * (j + 1))
+                d_cols = slice(TILE_COLS * c + BANK * j, TILE_COLS * c + BANK * (j + 1))
+                proj = work.tile([P, BANK], F32, tag="work")
+                for g in range(OUT_GROUPS):
+                    nc.tensor.matmul_mx(
+                        out=proj[:],
+                        lhsT=attn_codes[:, g, :].bitcast(FP8X4),
+                        lhsT_scale=attn_scales[:, g, :],
+                        rhs=weights[OUT_GROUPS * c + g][:, cols].bitcast(FP8X4),
+                        rhs_scale=out_planes[4 * c : P, g, cols],
+                        start=(g == 0),
+                        stop=(g == OUT_GROUPS - 1),
+                    )
+                nc.vector.tensor_tensor(
+                    out=x_mid[:, d_cols], in0=proj[:], in1=x_sb[:, d_cols], op=ALU.add
+                )
+            for j in range(BANKS_PER_TILE):
+                d_cols = slice(TILE_COLS * c + BANK * j, TILE_COLS * c + BANK * (j + 1))
+                nc.vector.bn_stats(out=stats[:, BANKS_PER_TILE * c + j, :], in_=x_mid[:, d_cols])
+            for g in range(OUT_GROUPS):
+                load_weight_tile(OUT_GROUPS * c + g + RING)
+
+        for c in range(OUT_QUARTERS):
+            d_cols = slice(TILE_COLS * c, TILE_COLS * (c + 1))
+            nc.sync.dma_start(out=x_mid_rows[:, d_cols], in_=x_mid[:, d_cols])
+
+        nc.vector.bn_aggr(out=mean_var[:], in_=stats[:].rearrange("p c s -> p (c s)"))
+        nc.vector.tensor_scalar_add(out=var_eps[:], in0=mean_var[:, 1:2], scalar1=EPS)
+        nc.scalar.activation(out=std[:], in_=var_eps[:], func=ACT.Sqrt)
+        nc.vector.reciprocal(out=rstd[:], in_=std[:])
+
+        def normalise(r):
+            tiles = []
+            for g in range(GROUPS_PER_ROUND * r, GROUPS_PER_ROUND * (r + 1)):
+                z = stage.tile([P, PACK, P], F32)
+                nc.vector.tensor_scalar(
+                    out=z[:],
+                    in0=x_mid[:, K_PASS * g : K_PASS * (g + 1)].rearrange("k (p t) -> k t p", t=PACK),
+                    scalar1=mean_var[:, 0:1],
+                    scalar2=rstd[:, 0:1],
+                    op0=ALU.subtract,
+                    op1=ALU.mult,
+                )
+                tiles.append(z)
+            return tiles
+
+        def transpose(tiles):
+            banks = []
+            for z in tiles:
+                z_t = work.tile([P, PACK, P], F32, tag="work")
+                for t in range(PACK):
+                    nc.tensor.transpose(out=z_t[:, t, :], in_=z[:, t, :], identity=ident[:])
+                banks.append(z_t)
+            return banks
+
+        def gain_bias_quantise(r, banks):
+            grouped_tiles = []
+            for i, z_t in enumerate(banks):
+                g = GROUPS_PER_ROUND * r + i
+                grouped = stage.tile([P, P, PACK], BF16, align_bytes=64)
+                for t in range(PACK):
+                    gain = gain_bias[:, g, t : t + 1]
+                    bias = gain_bias[:, FC1_GROUPS + g, t : t + 1]
+                    if g % 2 == 0:
+                        nc.scalar.activation(
+                            out=grouped[:, :, t], in_=z_t[:, t, :], func=ACT.Identity,
+                            scale=gain, bias=bias,
+                        )
+                    else:
+                        nc.vector.tensor_scalar(
+                            out=grouped[:, :, t], in0=z_t[:, t, :], scalar1=gain, scalar2=bias,
+                            op0=ALU.mult, op1=ALU.add,
+                        )
+                grouped_tiles.append(grouped)
+            for i, grouped in enumerate(grouped_tiles):
+                g = GROUPS_PER_ROUND * r + i
+                nc.vector.quantize_mx(
+                    out=h_codes[:, g, :].bitcast(FP8X4),
+                    scales=h_scales[:, g, :],
+                    in_=grouped[:].rearrange("p k t -> p (k t)"),
+                )
+
+        u_banks = [sums.tile([P, BANK], F32, name="u%d" % j) for j in range(F // BANK)]
+
+        def multiply(r):
+            for g in range(GROUPS_PER_ROUND * r, GROUPS_PER_ROUND * (r + 1)):
+                block, plane = divmod(g, PLANES)
+                for j in range(F // BANK):
+                    cols = slice(BANK * j, BANK * (j + 1))
+                    nc.tensor.matmul_mx(
+                        out=u_banks[j][:],
+                        lhsT=h_codes[:, g, :].bitcast(FP8X4),
+                        lhsT_scale=h_scales[:, g, :],
+                        rhs=weights[OUT_TILES + g][:, cols].bitcast(FP8X4),
+                        rhs_scale=fc1_planes[4 * plane : P, block, cols],
+                        start=(g == 0),
+                        stop=(g == FC1_GROUPS - 1),
+                    )
+
+        banks = transpose(normalise(0))
+        for r in range(ROUNDS):
+            if r + 1 < ROUNDS:
+                tiles = normalise(r + 1)
+            gain_bias_quantise(r, banks)
+            if r + 1 < ROUNDS:
+                banks = transpose(tiles)
+            multiply(r)
+
+        for j in range(F // BANK):
+            cols = slice(BANK * j, BANK * (j + 1))
+            nc.scalar.activation(out=act[:, cols], in_=u_banks[j][:], func=ACT.Gelu)
+            nc.sync.dma_start(out=act_rows[:, cols], in_=act[:, cols])

@@ -78,13 +78,7 @@ def tile_minitransformerlayer_pb_k_kernel(
         make_identity(nc, ident[:])
 
         nc.sync.dma_start(out=attn[:], in_=h_attn_rows)
-        nc.sync.dma_start(
-            out=gain_bias_rows[0:FC1_GROUPS, :], in_=g2.rearrange("(g k) -> g k", k=K_PASS)
-        )
-        nc.sync.dma_start(
-            out=gain_bias_rows[FC1_GROUPS : 2 * FC1_GROUPS, :],
-            in_=b2.rearrange("(g k) -> g k", k=K_PASS),
-        )
+        nc.sync.dma_start(out=x_sb[:], in_=x_rows)
         for g in range(OUT_GROUPS):
             for q in range(4):
                 nc.sync.dma_start(
@@ -93,13 +87,13 @@ def tile_minitransformerlayer_pb_k_kernel(
                     .rearrange("r (c n) -> c r n", c=PLANES)
                     .bitcast(I32),
                 )
-        for j in range(FC1_GROUPS // PLANES):
-            for q in range(4):
-                nc.sync.dma_start(
-                    out=fc1_planes[32 * q : 32 * q + 4 * PLANES, j, :].bitcast(I32),
-                    in_=w_fc1_scales[PLANES * j : PLANES * (j + 1), 4 * q : 4 * q + 4, :].bitcast(I32),
-                )
-        nc.sync.dma_start(out=x_sb[:], in_=x_rows)
+        nc.sync.dma_start(
+            out=gain_bias_rows[0:FC1_GROUPS, :], in_=g2.rearrange("(g k) -> g k", k=K_PASS)
+        )
+        nc.sync.dma_start(
+            out=gain_bias_rows[FC1_GROUPS : 2 * FC1_GROUPS, :],
+            in_=b2.rearrange("(g k) -> g k", k=K_PASS),
+        )
 
         weights = {}
 
@@ -115,7 +109,15 @@ def tile_minitransformerlayer_pb_k_kernel(
             nc.sync.dma_start(out=words[:].bitcast(I32), in_=source.bitcast(I32))
             weights[i] = words
 
-        for i in range(RING):
+        for i in range(OUT_TILES):
+            load_weight_tile(i)
+        for j in range(FC1_GROUPS // PLANES):
+            for q in range(4):
+                nc.sync.dma_start(
+                    out=fc1_planes[32 * q : 32 * q + 4 * PLANES, j, :].bitcast(I32),
+                    in_=w_fc1_scales[PLANES * j : PLANES * (j + 1), 4 * q : 4 * q + 4, :].bitcast(I32),
+                )
+        for i in range(OUT_TILES, RING):
             load_weight_tile(i)
 
         attn_words = attn[:].bitcast(F32)

@@ -77,6 +77,12 @@ def tile_minitransformerlayer_pb_k_kernel(
         nc.vector.memset(fc1_planes[:].bitcast(I32), 0)
         make_identity(nc, ident[:])
 
+        for j in range(FC1_GROUPS // PLANES):
+            for q in range(4):
+                nc.gpsimd.dma_start(
+                    out=fc1_planes[32 * q : 32 * q + 4 * PLANES, j, :].bitcast(F32),
+                    in_=w_fc1_scales[PLANES * j : PLANES * (j + 1), 4 * q : 4 * q + 4, :].bitcast(F32),
+                )
         nc.sync.dma_start(out=attn[:], in_=h_attn_rows)
         nc.sync.dma_start(out=x_sb[:], in_=x_rows)
         for g in range(OUT_GROUPS):
@@ -109,15 +115,7 @@ def tile_minitransformerlayer_pb_k_kernel(
             nc.sync.dma_start(out=words[:].bitcast(I32), in_=source.bitcast(I32))
             weights[i] = words
 
-        for i in range(OUT_TILES):
-            load_weight_tile(i)
-        for j in range(FC1_GROUPS // PLANES):
-            for q in range(4):
-                nc.sync.dma_start(
-                    out=fc1_planes[32 * q : 32 * q + 4 * PLANES, j, :].bitcast(I32),
-                    in_=w_fc1_scales[PLANES * j : PLANES * (j + 1), 4 * q : 4 * q + 4, :].bitcast(I32),
-                )
-        for i in range(OUT_TILES, RING):
+        for i in range(RING):
             load_weight_tile(i)
 
         attn_words = attn[:].bitcast(F32)

@@ -49,7 +49,7 @@ def tile_minitransformerlayer_pb_k_kernel(
         tc.tile_pool(name="ring", bufs=RING) as ring,
         tc.tile_pool(name="stage", bufs=GROUPS_PER_ROUND) as stage,
         tc.psum_pool(name="work", bufs=4) as work,
-        tc.psum_pool(name="sums", bufs=1) as sums,
+        tc.psum_pool(name="u_sums", bufs=1) as u_sums,
     ):
         ident = keep.tile([P, P], F32)
         attn = keep.tile([P, E], BF16)
@@ -63,8 +63,16 @@ def tile_minitransformerlayer_pb_k_kernel(
         gain_bias = keep.tile([P, 2 * FC1_GROUPS, PACK], F32)
         x_sb = keep.tile([P, D], BF16)
         x_mid = keep.tile([P, D], F32)
-        stats = keep.tile([P, D // BANK, 6], F32)
-        mean_var = keep.tile([P, 2], F32)
+        sums = keep.tile([P, D // BANK], F32)
+        squares = keep.tile([P, D // BANK], F32)
+        deviations = keep.tile([P, BANK], F32)
+        shift = keep.tile([P, 1], F32)
+        total = keep.tile([P, 1], F32)
+        total_squares = keep.tile([P, 1], F32)
+        mean = keep.tile([P, 1], F32)
+        offset = keep.tile([P, 1], F32)
+        offset_squared = keep.tile([P, 1], F32)
+        warm = keep.tile([P, 1], F32)
         var_eps = keep.tile([P, 1], F32)
         std = keep.tile([P, 1], F32)
         rstd = keep.tile([P, 1], F32)
@@ -72,10 +80,12 @@ def tile_minitransformerlayer_pb_k_kernel(
         h_scales = keep.tile([P, FC1_GROUPS, P], U8, align_bytes=64)
         act = keep.tile([P, F], F32)
 
+        nc.vector.memset(warm[:], 1.0)
         nc.vector.memset(gain_bias_rows[:], 0.0)
         nc.vector.memset(out_planes[:].bitcast(I32), 0)
         nc.vector.memset(fc1_planes[:].bitcast(I32), 0)
         make_identity(nc, ident[:])
+        nc.scalar.activation(out=std[:], in_=warm[:], func=ACT.Sqrt)
 
         for j in range(FC1_GROUPS // PLANES):
             for q in range(4):
@@ -164,12 +174,19 @@ def tile_minitransformerlayer_pb_k_kernel(
                         start=(g == 0),
                         stop=(g == OUT_GROUPS - 1),
                     )
-                nc.vector.tensor_tensor(
-                    out=x_mid[:, d_cols], in0=proj[:], in1=x_sb[:, d_cols], op=ALU.add
+                i = BANKS_PER_TILE * c + j
+                nc.vector.scalar_tensor_tensor(
+                    out=x_mid[:, d_cols], in0=proj[:], scalar=1.0, in1=x_sb[:, d_cols],
+                    op0=ALU.mult, op1=ALU.add, accum_out=sums[:, i : i + 1],
                 )
-            for j in range(BANKS_PER_TILE):
-                d_cols = slice(TILE_COLS * c + BANK * j, TILE_COLS * c + BANK * (j + 1))
-                nc.vector.bn_stats(out=stats[:, BANKS_PER_TILE * c + j, :], in_=x_mid[:, d_cols])
+                if i == 0:
+                    nc.vector.tensor_scalar_mul(
+                        out=shift[:], in0=sums[:, 0:1], scalar1=-1.0 / BANK
+                    )
+                nc.scalar.activation(
+                    out=deviations[:], in_=x_mid[:, d_cols], func=ACT.Square,
+                    bias=shift[:], accum_out=squares[:, i : i + 1],
+                )
             for g in range(OUT_GROUPS):
                 load_weight_tile(OUT_GROUPS * c + g + RING)
 
@@ -177,8 +194,21 @@ def tile_minitransformerlayer_pb_k_kernel(
             d_cols = slice(TILE_COLS * c, TILE_COLS * (c + 1))
             nc.sync.dma_start(out=x_mid_rows[:, d_cols], in_=x_mid[:, d_cols])
 
-        nc.vector.bn_aggr(out=mean_var[:], in_=stats[:].rearrange("p c s -> p (c s)"))
-        nc.vector.tensor_scalar_add(out=var_eps[:], in0=mean_var[:, 1:2], scalar1=EPS)
+        nc.vector.reduce_sum(out=total[:], in_=sums[:], axis=mybir.AxisListType.X)
+        nc.vector.tensor_scalar_mul(out=mean[:], in0=total[:], scalar1=1.0 / D)
+        nc.vector.tensor_scalar(
+            out=offset[:], in0=total[:], scalar1=1.0 / D, scalar2=shift[:, 0:1],
+            op0=ALU.mult, op1=ALU.add,
+        )
+        nc.vector.tensor_scalar(
+            out=offset_squared[:], in0=offset[:], scalar1=offset[:, 0:1], scalar2=-EPS,
+            op0=ALU.mult, op1=ALU.add,
+        )
+        nc.vector.reduce_sum(out=total_squares[:], in_=squares[:], axis=mybir.AxisListType.X)
+        nc.vector.scalar_tensor_tensor(
+            out=var_eps[:], in0=total_squares[:], scalar=1.0 / D, in1=offset_squared[:],
+            op0=ALU.mult, op1=ALU.subtract,
+        )
         nc.scalar.activation(out=std[:], in_=var_eps[:], func=ACT.Sqrt)
         nc.vector.reciprocal(out=rstd[:], in_=std[:])
 
@@ -189,7 +219,7 @@ def tile_minitransformerlayer_pb_k_kernel(
                 nc.vector.tensor_scalar(
                     out=z[:],
                     in0=x_mid[:, K_PASS * g : K_PASS * (g + 1)].rearrange("k (p t) -> k t p", t=PACK),
-                    scalar1=mean_var[:, 0:1],
+                    scalar1=mean[:, 0:1],
                     scalar2=rstd[:, 0:1],
                     op0=ALU.subtract,
                     op1=ALU.mult,
@@ -233,7 +263,7 @@ def tile_minitransformerlayer_pb_k_kernel(
                     in_=grouped[:].rearrange("p k t -> p (k t)"),
                 )
 
-        u_banks = [sums.tile([P, BANK], F32, name="u%d" % j) for j in range(F // BANK)]
+        u_banks = [u_sums.tile([P, BANK], F32, name="u%d" % j) for j in range(F // BANK)]
 
         def multiply(r):
             for g in range(GROUPS_PER_ROUND * r, GROUPS_PER_ROUND * (r + 1)):

@@ -21,11 +21,12 @@ BANK = 512
 OUT_GROUPS = E // K_PASS
 FC1_GROUPS = D // K_PASS
 TILE_COLS = 2048
+TILE_GROUPS = 2
 BANKS_PER_TILE = TILE_COLS // BANK
-OUT_QUARTERS = D // TILE_COLS
-OUT_TILES = OUT_QUARTERS * OUT_GROUPS
-ALL_TILES = OUT_TILES + FC1_GROUPS
-RING = 16
+OUT_TILES = D // TILE_COLS
+FC1_TILES = FC1_GROUPS // TILE_GROUPS
+ALL_TILES = OUT_TILES + FC1_TILES
+RING = 8
 assert OUT_TILES + RING == ALL_TILES
 PLANES = 4
 GROUPS_PER_ROUND = 4
@@ -114,14 +115,14 @@ def tile_minitransformerlayer_pb_k_kernel(
         weights = {}
 
         def load_weight_tile(i):
-            words = ring.tile([P, TILE_COLS], U32, align_bytes=64)
+            words = ring.tile([P, TILE_GROUPS, TILE_COLS], U32, align_bytes=64)
             if i < OUT_TILES:
-                c, g = divmod(i, OUT_GROUPS)
-                source = w_out_words[g].rearrange("p n t -> p (n t)")[
-                    :, PACK * TILE_COLS * c : PACK * TILE_COLS * (c + 1)
+                source = w_out_words.rearrange("g p n t -> p g (n t)")[
+                    :, :, PACK * TILE_COLS * i : PACK * TILE_COLS * (i + 1)
                 ]
             else:
-                source = w_fc1_words[i - OUT_TILES].rearrange("p n t -> p (n t)")
+                first = TILE_GROUPS * (i - OUT_TILES)
+                source = w_fc1_words[first : first + TILE_GROUPS].rearrange("g p n t -> p g (n t)")
             nc.sync.dma_start(out=words[:].bitcast(I32), in_=source.bitcast(I32))
             weights[i] = words
 
@@ -159,7 +160,7 @@ def tile_minitransformerlayer_pb_k_kernel(
             in_=gain_bias_t[:, :, 0 : 2 * FC1_GROUPS].rearrange("p t r -> p r t"),
         )
 
-        for c in range(OUT_QUARTERS):
+        for c in range(OUT_TILES):
             for j in range(BANKS_PER_TILE):
                 cols = slice(BANK * j, BANK * (j + 1))
                 d_cols = slice(TILE_COLS * c + BANK * j, TILE_COLS * c + BANK * (j + 1))
@@ -169,7 +170,7 @@ def tile_minitransformerlayer_pb_k_kernel(
                         out=proj[:],
                         lhsT=attn_codes[:, g, :].bitcast(FP8X4),
                         lhsT_scale=attn_scales[:, g, :],
-                        rhs=weights[OUT_GROUPS * c + g][:, cols].bitcast(FP8X4),
+                        rhs=weights[c][:, g, cols].bitcast(FP8X4),
                         rhs_scale=out_planes[4 * c : P, g, cols],
                         start=(g == 0),
                         stop=(g == OUT_GROUPS - 1),
@@ -187,11 +188,10 @@ def tile_minitransformerlayer_pb_k_kernel(
                     out=deviations[:], in_=x_mid[:, d_cols], func=ACT.Square,
                     bias=shift[:], accum_out=squares[:, i : i + 1],
                 )
-            for g in range(OUT_GROUPS):
-                load_weight_tile(OUT_GROUPS * c + g + RING)
+            load_weight_tile(c + RING)
 
-        for c in range(OUT_QUARTERS):
-            d_cols = slice(TILE_COLS * c, TILE_COLS * (c + 1))
+        for half in range(2):
+            d_cols = slice(D // 2 * half, D // 2 * (half + 1))
             nc.sync.dma_start(out=x_mid_rows[:, d_cols], in_=x_mid[:, d_cols])
 
         nc.vector.reduce_sum(out=total[:], in_=sums[:], axis=mybir.AxisListType.X)
@@ -274,7 +274,7 @@ def tile_minitransformerlayer_pb_k_kernel(
                         out=u_banks[j][:],
                         lhsT=h_codes[:, g, :].bitcast(FP8X4),
                         lhsT_scale=h_scales[:, g, :],
-                        rhs=weights[OUT_TILES + g][:, cols].bitcast(FP8X4),
+                        rhs=weights[OUT_TILES + g // TILE_GROUPS][:, g % TILE_GROUPS, cols].bitcast(FP8X4),
                         rhs_scale=fc1_planes[4 * plane : P, block, cols],
                         start=(g == 0),
                         stop=(g == FC1_GROUPS - 1),
@@ -292,4 +292,6 @@ def tile_minitransformerlayer_pb_k_kernel(
         for j in range(F // BANK):
             cols = slice(BANK * j, BANK * (j + 1))
             nc.scalar.activation(out=act[:, cols], in_=u_banks[j][:], func=ACT.Gelu)
+        for half in range(2):
+            cols = slice(F // 2 * half, F // 2 * (half + 1))
             nc.sync.dma_start(out=act_rows[:, cols], in_=act[:, cols])

@@ -21,13 +21,14 @@ BANK = 512
 OUT_GROUPS = E // K_PASS
 FC1_GROUPS = D // K_PASS
 TILE_COLS = 2048
-TILE_GROUPS = 2
-BANKS_PER_TILE = TILE_COLS // BANK
-OUT_TILES = D // TILE_COLS
+TILE_GROUPS = 4
+OUT_RANGES = D // TILE_COLS
+RANGES_PER_TILE = TILE_GROUPS // OUT_GROUPS
+OUT_TILES = OUT_RANGES // RANGES_PER_TILE
 FC1_TILES = FC1_GROUPS // TILE_GROUPS
-ALL_TILES = OUT_TILES + FC1_TILES
-RING = 8
-assert OUT_TILES + RING == ALL_TILES
+BANKS_PER_RANGE = TILE_COLS // BANK
+RING = 4
+assert OUT_TILES + RING == OUT_TILES + FC1_TILES
 PLANES = 4
 GROUPS_PER_ROUND = 4
 ROUNDS = FC1_GROUPS // GROUPS_PER_ROUND
@@ -112,22 +113,29 @@ def tile_minitransformerlayer_pb_k_kernel(
             in_=b2.rearrange("(g k) -> g k", k=K_PASS),
         )
 
-        weights = {}
-
-        def load_weight_tile(i):
-            words = ring.tile([P, TILE_GROUPS, TILE_COLS], U32, align_bytes=64)
-            if i < OUT_TILES:
+        out_ranges = []
+        for tile_index in range(OUT_TILES):
+            words = ring.tile([P, RANGES_PER_TILE, OUT_GROUPS, TILE_COLS], U32, name="words", tag="words", align_bytes=64)
+            for i in range(RANGES_PER_TILE):
+                c = RANGES_PER_TILE * tile_index + i
                 source = w_out_words.rearrange("g p n t -> p g (n t)")[
-                    :, :, PACK * TILE_COLS * i : PACK * TILE_COLS * (i + 1)
+                    :, :, PACK * TILE_COLS * c : PACK * TILE_COLS * (c + 1)
                 ]
-            else:
-                first = TILE_GROUPS * (i - OUT_TILES)
-                source = w_fc1_words[first : first + TILE_GROUPS].rearrange("g p n t -> p g (n t)")
-            nc.sync.dma_start(out=words[:].bitcast(I32), in_=source.bitcast(I32))
-            weights[i] = words
+                nc.sync.dma_start(out=words[:, i, :, :].bitcast(I32), in_=source.bitcast(I32))
+                out_ranges.append(words[:, i, :, :])
 
-        for i in range(RING):
-            load_weight_tile(i)
+        fc1_tiles = []
+
+        def load_fc1_tile(i):
+            words = ring.tile([P, TILE_GROUPS, TILE_COLS], U32, name="words", tag="words", align_bytes=64)
+            source = w_fc1_words[TILE_GROUPS * i : TILE_GROUPS * (i + 1)].rearrange(
+                "g p n t -> p g (n t)"
+            )
+            nc.sync.dma_start(out=words[:].bitcast(I32), in_=source.bitcast(I32))
+            fc1_tiles.append(words)
+
+        for i in range(RING - OUT_TILES):
+            load_fc1_tile(i)
 
         attn_words = attn[:].bitcast(F32)
         attn_t = work.tile([P, OUT_GROUPS, 2, P], F32, tag="work")
@@ -160,8 +168,8 @@ def tile_minitransformerlayer_pb_k_kernel(
             in_=gain_bias_t[:, :, 0 : 2 * FC1_GROUPS].rearrange("p t r -> p r t"),
         )
 
-        for c in range(OUT_TILES):
-            for j in range(BANKS_PER_TILE):
+        for c in range(OUT_RANGES):
+            for j in range(BANKS_PER_RANGE):
                 cols = slice(BANK * j, BANK * (j + 1))
                 d_cols = slice(TILE_COLS * c + BANK * j, TILE_COLS * c + BANK * (j + 1))
                 proj = work.tile([P, BANK], F32, tag="work")
@@ -170,12 +178,12 @@ def tile_minitransformerlayer_pb_k_kernel(
                         out=proj[:],
                         lhsT=attn_codes[:, g, :].bitcast(FP8X4),
                         lhsT_scale=attn_scales[:, g, :],
-                        rhs=weights[c][:, g, cols].bitcast(FP8X4),
+                        rhs=out_ranges[c][:, g, cols].bitcast(FP8X4),
                         rhs_scale=out_planes[4 * c : P, g, cols],
                         start=(g == 0),
                         stop=(g == OUT_GROUPS - 1),
                     )
-                i = BANKS_PER_TILE * c + j
+                i = BANKS_PER_RANGE * c + j
                 nc.vector.scalar_tensor_tensor(
                     out=x_mid[:, d_cols], in0=proj[:], scalar=1.0, in1=x_sb[:, d_cols],
                     op0=ALU.mult, op1=ALU.add, accum_out=sums[:, i : i + 1],
@@ -188,11 +196,10 @@ def tile_minitransformerlayer_pb_k_kernel(
                     out=deviations[:], in_=x_mid[:, d_cols], func=ACT.Square,
                     bias=shift[:], accum_out=squares[:, i : i + 1],
                 )
-            load_weight_tile(c + RING)
+            if (c + 1) % RANGES_PER_TILE == 0:
+                load_fc1_tile(RING - OUT_TILES + c // RANGES_PER_TILE)
 
-        for half in range(2):
-            d_cols = slice(D // 2 * half, D // 2 * (half + 1))
-            nc.sync.dma_start(out=x_mid_rows[:, d_cols], in_=x_mid[:, d_cols])
+        nc.sync.dma_start(out=x_mid_rows, in_=x_mid[:])
 
         nc.vector.reduce_sum(out=total[:], in_=sums[:], axis=mybir.AxisListType.X)
         nc.vector.tensor_scalar_mul(out=mean[:], in0=total[:], scalar1=1.0 / D)
@@ -274,7 +281,7 @@ def tile_minitransformerlayer_pb_k_kernel(
                         out=u_banks[j][:],
                         lhsT=h_codes[:, g, :].bitcast(FP8X4),
                         lhsT_scale=h_scales[:, g, :],
-                        rhs=weights[OUT_TILES + g // TILE_GROUPS][:, g % TILE_GROUPS, cols].bitcast(FP8X4),
+                        rhs=fc1_tiles[g // TILE_GROUPS][:, g % TILE_GROUPS, cols].bitcast(FP8X4),
                         rhs_scale=fc1_planes[4 * plane : P, block, cols],
                         start=(g == 0),
                         stop=(g == FC1_GROUPS - 1),
@@ -292,6 +299,4 @@ def tile_minitransformerlayer_pb_k_kernel(
         for j in range(F // BANK):
             cols = slice(BANK * j, BANK * (j + 1))
             nc.scalar.activation(out=act[:, cols], in_=u_banks[j][:], func=ACT.Gelu)
-        for half in range(2):
-            cols = slice(F // 2 * half, F // 2 * (half + 1))
-            nc.sync.dma_start(out=act_rows[:, cols], in_=act[:, cols])
+        nc.sync.dma_start(out=act_rows, in_=act[:])

import concourse.mybir as mybir
from concourse.masks import make_identity

F32 = mybir.dt.float32
BF16 = mybir.dt.bfloat16
U8 = mybir.dt.uint8
U32 = mybir.dt.uint32
I32 = mybir.dt.int32
FP8X4 = mybir.dt.float8_e4m3fn_x4
ALU = mybir.AluOpType
ACT = mybir.ActivationFunctionType

P = 128
PACK = 4
K_PASS = P * PACK
E = 1024
D = 8192
F = 2048
EPS = 1e-5
BANK = 512
OUT_GROUPS = E // K_PASS
FC1_GROUPS = D // K_PASS
TILE_COLS = 2048
TILE_GROUPS = 4
OUT_RANGES = D // TILE_COLS
RANGES_PER_TILE = TILE_GROUPS // OUT_GROUPS
OUT_TILES = OUT_RANGES // RANGES_PER_TILE
FC1_TILES = FC1_GROUPS // TILE_GROUPS
BANKS_PER_RANGE = TILE_COLS // BANK
RING = 4
assert OUT_TILES + RING == OUT_TILES + FC1_TILES
PLANES = 4
GROUPS_PER_ROUND = 4
ROUNDS = FC1_GROUPS // GROUPS_PER_ROUND

FLOPS = 2 * P * E * D + 2 * P * D * F


def tile_minitransformerlayer_pb_k_kernel(
    tc, h_attn, x, w_out_words, w_out_scales, w_fc1_words, w_fc1_scales, g2, b2, out_0, out_1
):
    nc = tc.nc
    h_attn_rows = h_attn.flatten_outer_dims()
    x_rows = x.flatten_outer_dims()
    x_mid_rows = out_0.flatten_outer_dims()
    act_rows = out_1.flatten_outer_dims()

    with (
        tc.manual_schedule(),
        tc.tile_pool(name="keep", bufs=1) as keep,
        tc.tile_pool(name="ring", bufs=RING) as ring,
        tc.tile_pool(name="stage", bufs=GROUPS_PER_ROUND) as stage,
        tc.psum_pool(name="work", bufs=4) as work,
        tc.psum_pool(name="u_sums", bufs=1) as u_sums,
    ):
        ident = keep.tile([P, P], F32)
        attn = keep.tile([P, E], BF16)
        attn_grouped = keep.tile([P, OUT_GROUPS, P, PACK], BF16, align_bytes=64)
        attn_codes = keep.tile([P, OUT_GROUPS, P], U32, align_bytes=64)
        attn_scales = keep.tile([P, OUT_GROUPS, P], U8, align_bytes=64)
        out_planes = keep.tile([P, OUT_GROUPS, TILE_COLS], U8, align_bytes=64)
        fc1_planes = keep.tile([P, FC1_GROUPS // PLANES, F], U8, align_bytes=64)
        gain_bias_rows = keep.tile([P, K_PASS], BF16)
        gain_bias_sorted = keep.tile([P, PACK, P], F32)
        gain_bias = keep.tile([P, 2 * FC1_GROUPS, PACK], F32)
        x_sb = keep.tile([P, D], BF16)
        x_mid = keep.tile([P, D], F32)
        sums = keep.tile([P, D // BANK], F32)
        squares = keep.tile([P, D // BANK], F32)
        deviations = keep.tile([P, BANK], F32)
        shift = keep.tile([P, 1], F32)
        total = keep.tile([P, 1], F32)
        total_squares = keep.tile([P, 1], F32)
        mean = keep.tile([P, 1], F32)
        offset = keep.tile([P, 1], F32)
        offset_squared = keep.tile([P, 1], F32)
        warm = keep.tile([P, 1], F32)
        var_eps = keep.tile([P, 1], F32)
        std = keep.tile([P, 1], F32)
        rstd = keep.tile([P, 1], F32)
        h_codes = keep.tile([P, FC1_GROUPS, P], U32, align_bytes=64)
        h_scales = keep.tile([P, FC1_GROUPS, P], U8, align_bytes=64)
        act = keep.tile([P, F], F32)

        nc.vector.memset(warm[:], 1.0)
        nc.vector.memset(gain_bias_rows[:], 0.0)
        nc.vector.memset(out_planes[:].bitcast(I32), 0)
        nc.vector.memset(fc1_planes[:].bitcast(I32), 0)
        make_identity(nc, ident[:])
        nc.scalar.activation(out=std[:], in_=warm[:], func=ACT.Sqrt)

        for j in range(FC1_GROUPS // PLANES):
            for q in range(4):
                nc.gpsimd.dma_start(
                    out=fc1_planes[32 * q : 32 * q + 4 * PLANES, j, :].bitcast(F32),
                    in_=w_fc1_scales[PLANES * j : PLANES * (j + 1), 4 * q : 4 * q + 4, :].bitcast(F32),
                )
        nc.sync.dma_start(out=attn[:], in_=h_attn_rows)
        nc.sync.dma_start(out=x_sb[:], in_=x_rows)
        for g in range(OUT_GROUPS):
            for q in range(4):
                nc.sync.dma_start(
                    out=out_planes[32 * q : 32 * q + 4 * PLANES, g, :].bitcast(I32),
                    in_=w_out_scales[g, 4 * q : 4 * q + 4, :]
                    .rearrange("r (c n) -> c r n", c=PLANES)
                    .bitcast(I32),
                )
        nc.sync.dma_start(
            out=gain_bias_rows[0:FC1_GROUPS, :], in_=g2.rearrange("(g k) -> g k", k=K_PASS)
        )
        nc.sync.dma_start(
            out=gain_bias_rows[FC1_GROUPS : 2 * FC1_GROUPS, :],
            in_=b2.rearrange("(g k) -> g k", k=K_PASS),
        )

        out_ranges = []
        for tile_index in range(OUT_TILES):
            words = ring.tile([P, RANGES_PER_TILE, OUT_GROUPS, TILE_COLS], U32, name="words", tag="words", align_bytes=64)
            for i in range(RANGES_PER_TILE):
                c = RANGES_PER_TILE * tile_index + i
                source = w_out_words.rearrange("g p n t -> p g (n t)")[
                    :, :, PACK * TILE_COLS * c : PACK * TILE_COLS * (c + 1)
                ]
                nc.sync.dma_start(out=words[:, i, :, :].bitcast(I32), in_=source.bitcast(I32))
                out_ranges.append(words[:, i, :, :])

        fc1_tiles = []

        def load_fc1_tile(i):
            words = ring.tile([P, TILE_GROUPS, TILE_COLS], U32, name="words", tag="words", align_bytes=64)
            source = w_fc1_words[TILE_GROUPS * i : TILE_GROUPS * (i + 1)].rearrange(
                "g p n t -> p g (n t)"
            )
            nc.sync.dma_start(out=words[:].bitcast(I32), in_=source.bitcast(I32))
            fc1_tiles.append(words)

        for i in range(RING - OUT_TILES):
            load_fc1_tile(i)

        attn_words = attn[:].bitcast(F32)
        attn_t = work.tile([P, OUT_GROUPS, 2, P], F32, tag="work")
        for g in range(OUT_GROUPS):
            for u in range(2):
                nc.tensor.transpose(
                    out=attn_t[:, g, u, :],
                    in_=attn_words[:, 256 * g + u : 256 * (g + 1) : 2],
                    identity=ident[:],
                )
        nc.vector.tensor_copy(
            out=attn_grouped[:].bitcast(F32), in_=attn_t[:].rearrange("p g u k -> p g k u")
        )

        nc.vector.tensor_copy(
            out=gain_bias_sorted[:], in_=gain_bias_rows[:].rearrange("r (p t) -> r t p", t=PACK)
        )
        nc.vector.quantize_mx(
            out=attn_codes[:].rearrange("p g k -> p (g k)").bitcast(FP8X4),
            scales=attn_scales[:].rearrange("p g k -> p (g k)"),
            in_=attn_grouped[:].rearrange("p g k t -> p (g k t)"),
        )
        gain_bias_t = work.tile([P, PACK, P], F32, tag="work")
        for t in range(PACK):
            nc.tensor.transpose(
                out=gain_bias_t[:, t, :], in_=gain_bias_sorted[:, t, :], identity=ident[:]
            )
        nc.vector.tensor_copy(
            out=gain_bias[:],
            in_=gain_bias_t[:, :, 0 : 2 * FC1_GROUPS].rearrange("p t r -> p r t"),
        )

        for c in range(OUT_RANGES):
            for j in range(BANKS_PER_RANGE):
                cols = slice(BANK * j, BANK * (j + 1))
                d_cols = slice(TILE_COLS * c + BANK * j, TILE_COLS * c + BANK * (j + 1))
                proj = work.tile([P, BANK], F32, tag="work")
                for g in range(OUT_GROUPS):
                    nc.tensor.matmul_mx(
                        out=proj[:],
                        lhsT=attn_codes[:, g, :].bitcast(FP8X4),
                        lhsT_scale=attn_scales[:, g, :],
                        rhs=out_ranges[c][:, g, cols].bitcast(FP8X4),
                        rhs_scale=out_planes[4 * c : P, g, cols],
                        start=(g == 0),
                        stop=(g == OUT_GROUPS - 1),
                    )
                i = BANKS_PER_RANGE * c + j
                nc.vector.scalar_tensor_tensor(
                    out=x_mid[:, d_cols], in0=proj[:], scalar=1.0, in1=x_sb[:, d_cols],
                    op0=ALU.mult, op1=ALU.add, accum_out=sums[:, i : i + 1],
                )
                if i == 0:
                    nc.vector.tensor_scalar_mul(
                        out=shift[:], in0=sums[:, 0:1], scalar1=-1.0 / BANK
                    )
                nc.scalar.activation(
                    out=deviations[:], in_=x_mid[:, d_cols], func=ACT.Square,
                    bias=shift[:], accum_out=squares[:, i : i + 1],
                )
            if (c + 1) % RANGES_PER_TILE == 0:
                load_fc1_tile(RING - OUT_TILES + c // RANGES_PER_TILE)

        nc.sync.dma_start(out=x_mid_rows, in_=x_mid[:])

        nc.vector.reduce_sum(out=total[:], in_=sums[:], axis=mybir.AxisListType.X)
        nc.vector.tensor_scalar_mul(out=mean[:], in0=total[:], scalar1=1.0 / D)
        nc.vector.tensor_scalar(
            out=offset[:], in0=total[:], scalar1=1.0 / D, scalar2=shift[:, 0:1],
            op0=ALU.mult, op1=ALU.add,
        )
        nc.vector.tensor_scalar(
            out=offset_squared[:], in0=offset[:], scalar1=offset[:, 0:1], scalar2=-EPS,
            op0=ALU.mult, op1=ALU.add,
        )
        nc.vector.reduce_sum(out=total_squares[:], in_=squares[:], axis=mybir.AxisListType.X)
        nc.vector.scalar_tensor_tensor(
            out=var_eps[:], in0=total_squares[:], scalar=1.0 / D, in1=offset_squared[:],
            op0=ALU.mult, op1=ALU.subtract,
        )
        nc.scalar.activation(out=std[:], in_=var_eps[:], func=ACT.Sqrt)
        nc.vector.reciprocal(out=rstd[:], in_=std[:])

        def normalise(r):
            tiles = []
            for g in range(GROUPS_PER_ROUND * r, GROUPS_PER_ROUND * (r + 1)):
                z = stage.tile([P, PACK, P], F32)
                nc.vector.tensor_scalar(
                    out=z[:],
                    in0=x_mid[:, K_PASS * g : K_PASS * (g + 1)].rearrange("k (p t) -> k t p", t=PACK),
                    scalar1=mean[:, 0:1],
                    scalar2=rstd[:, 0:1],
                    op0=ALU.subtract,
                    op1=ALU.mult,
                )
                tiles.append(z)
            return tiles

        def transpose(tiles):
            banks = []
            for z in tiles:
                z_t = work.tile([P, PACK, P], F32, tag="work")
                for t in range(PACK):
                    nc.tensor.transpose(out=z_t[:, t, :], in_=z[:, t, :], identity=ident[:])
                banks.append(z_t)
            return banks

        def gain_bias_quantise(r, banks):
            grouped_tiles = []
            for i, z_t in enumerate(banks):
                g = GROUPS_PER_ROUND * r + i
                grouped = stage.tile([P, P, PACK], BF16, align_bytes=64)
                for t in range(PACK):
                    gain = gain_bias[:, g, t : t + 1]
                    bias = gain_bias[:, FC1_GROUPS + g, t : t + 1]
                    if g % 2 == 0:
                        nc.scalar.activation(
                            out=grouped[:, :, t], in_=z_t[:, t, :], func=ACT.Identity,
                            scale=gain, bias=bias,
                        )
                    else:
                        nc.vector.tensor_scalar(
                            out=grouped[:, :, t], in0=z_t[:, t, :], scalar1=gain, scalar2=bias,
                            op0=ALU.mult, op1=ALU.add,
                        )
                grouped_tiles.append(grouped)
            for i, grouped in enumerate(grouped_tiles):
                g = GROUPS_PER_ROUND * r + i
                nc.vector.quantize_mx(
                    out=h_codes[:, g, :].bitcast(FP8X4),
                    scales=h_scales[:, g, :],
                    in_=grouped[:].rearrange("p k t -> p (k t)"),
                )

        u_banks = [u_sums.tile([P, BANK], F32, name="u%d" % j) for j in range(F // BANK)]

        def multiply(r):
            for g in range(GROUPS_PER_ROUND * r, GROUPS_PER_ROUND * (r + 1)):
                block, plane = divmod(g, PLANES)
                for j in range(F // BANK):
                    cols = slice(BANK * j, BANK * (j + 1))
                    nc.tensor.matmul_mx(
                        out=u_banks[j][:],
                        lhsT=h_codes[:, g, :].bitcast(FP8X4),
                        lhsT_scale=h_scales[:, g, :],
                        rhs=fc1_tiles[g // TILE_GROUPS][:, g % TILE_GROUPS, cols].bitcast(FP8X4),
                        rhs_scale=fc1_planes[4 * plane : P, block, cols],
                        start=(g == 0),
                        stop=(g == FC1_GROUPS - 1),
                    )

        banks = transpose(normalise(0))
        for r in range(ROUNDS):
            if r + 1 < ROUNDS:
                tiles = normalise(r + 1)
            gain_bias_quantise(r, banks)
            if r + 1 < ROUNDS:
                banks = transpose(tiles)
            multiply(r)

        for j in range(F // BANK):
            cols = slice(BANK * j, BANK * (j + 1))
            nc.scalar.activation(out=act[:, cols], in_=u_banks[j][:], func=ACT.Gelu)
        nc.sync.dma_start(out=act_rows, in_=act[:])
